import numpy as np
import ml_dtypes

BF16 = ml_dtypes.bfloat16


def bf(x):
    return np.asarray(x, np.float32).astype(BF16)


def f32(x):
    return np.asarray(x, np.float32)


def f64(x):
    return np.asarray(x).astype(np.float64)


def striped(idx):
    return np.tile(idx.reshape(-1, 16).T, (8, 1))


S, D, M, B, T, N = 1024, 128, 128, 128, 8, 1024
SCALE = np.sqrt(D)


def position_code():
    place = np.arange(T - 1, -1, -1).astype(np.float64)
    inv_freq = 1.0 / 10000.0 ** (np.arange(0.0, D, 2.0) / D)
    si = inv_freq[:, None] * place[None, :]
    return np.tile(np.concatenate([np.sin(si), np.cos(si)], axis=0), (1, B))


def setup_inputs():
    return {"table": bf(0.1 * np.random.standard_normal((D, S))), "w": bf(np.random.standard_normal((D, M)) / np.sqrt(D)), "pos": f32(position_code()), "mem_norm": f32(T * (0.5 + np.random.uniform(size=(M, B)))), "offs": striped(np.random.permutation(np.tile(np.arange(S), 2))[:N])}


def reference(table, w, pos, mem_norm, offs):
    idx = offs[:16].T.reshape(-1)
    v = SCALE * (f64(w).T @ f64(table)[:, idx]) + f64(w).T @ f64(pos)
    ck = np.exp(np.minimum(v, 0.0)) + np.maximum(v, 0.0)
    return f64(mem_norm) + ck.reshape(M, B, T).sum(axis=2)

@@ -1,0 +1,72 @@
+import math
+
+import concourse.mybir as mybir
+
+BF16, F32, U16 = mybir.dt.bfloat16, mybir.dt.float32, mybir.dt.uint16
+ALU = mybir.AluOpType
+ACT = mybir.ActivationFunctionType
+
+P = 128
+WORDS = 1024
+N = 1024
+T = 8
+PIECE = 512
+PIECES = N // PIECE
+SCALE = math.sqrt(128.0)
+
+FLOPS = 2 * (2 * P * P * N)
+
+
+def tile_infiniattentionlm_kernel(tc, table, w, pos, mem_norm, offs, out):
+    nc = tc.nc
+    with (
+        tc.tile_pool(name="held", bufs=1) as held,
+        tc.tile_pool(name="work", bufs=PIECES) as work,
+        tc.psum_pool(name="psum", bufs=PIECES) as psum,
+    ):
+        offsets = held.tile([P, N // 16], U16, name="offsets")
+        nc.sync.dma_start(offsets[:], offs)
+        words = held.tile([P, WORDS], BF16, name="words")
+        nc.sync.dma_start(words[:], table)
+        weights = held.tile([P, P], BF16, name="weights")
+        nc.scalar.dma_start(weights[:], w)
+        code = held.tile([P, N], F32, name="code")
+        nc.scalar.dma_start(code[:], pos)
+        old_norm = held.tile([P, N // T], F32, name="old_norm")
+        nc.gpsimd.dma_start(old_norm[:], mem_norm)
+        new_norm = held.tile([P, N // T], F32, name="new_norm")
+
+        scaled = []
+        for c in range(PIECES):
+            picked = psum.tile([P, PIECE], F32, name="picked")
+            piece_offsets = offsets[:, c * (PIECE // 16) : (c + 1) * (PIECE // 16)]
+            nc.tensor.matmul(picked[:], weights[:], words[:].indirect(piece_offsets), start=True, stop=True)
+            scaled_c = work.tile([P, PIECE], F32, name="scaled")
+            nc.scalar.mul(scaled_c[:], picked[:], SCALE)
+            scaled.append(scaled_c)
+
+        for c in range(PIECES):
+            entries = slice(c * PIECE, (c + 1) * PIECE)
+            sequences = slice(c * (PIECE // T), (c + 1) * (PIECE // T))
+            code_bf = work.tile([P, PIECE], BF16, name="code_bf")
+            nc.vector.tensor_copy(code_bf[:], code[:, entries])
+            placed = psum.tile([P, PIECE], F32, name="placed")
+            nc.tensor.matmul(placed[:], weights[:], code_bf[:], start=True, stop=True)
+            v = work.tile([P, PIECE], F32, name="v")
+            nc.vector.tensor_tensor(v[:], scaled[c][:], placed[:], ALU.add)
+            below = work.tile([P, PIECE], F32, name="below")
+            nc.vector.tensor_scalar_min(below[:], v[:], 0.0)
+            decayed = work.tile([P, PIECE], F32, name="decayed")
+            nc.scalar.activation(decayed[:], below[:], ACT.Exp)
+            feature = work.tile([P, PIECE], F32, name="feature")
+            nc.vector.scalar_tensor_tensor(feature[:], v[:], 0.0, decayed[:], ALU.max, ALU.add)
+            summed = work.tile([P, PIECE // T], F32, name="summed")
+            nc.vector.tensor_reduce(
+                out=summed[:],
+                in_=feature[:].rearrange("p (b t) -> p b t", t=T),
+                axis=mybir.AxisListType.X,
+                op=ALU.add,
+            )
+            nc.vector.tensor_tensor(new_norm[:, sequences], summed[:], old_norm[:, sequences], ALU.add)
+
+        nc.sync.dma_start(out, new_norm[:])

@@ -10,9 +10,11 @@ P = 128
 WORDS = 1024
 N = 1024
 T = 8
-PIECE = 512
+PIECE = 256
 PIECES = N // PIECE
 SCALE = math.sqrt(128.0)
+WARM_COLUMNS = 512
+WARM_MATMULS = 5
 
 FLOPS = 2 * (2 * P * P * N)
 
@@ -22,44 +24,64 @@ def tile_infiniattentionlm_kernel(tc, table, w, pos, mem_norm, offs, out):
     with (
         tc.tile_pool(name="held", bufs=1) as held,
         tc.tile_pool(name="work", bufs=PIECES) as work,
-        tc.psum_pool(name="psum", bufs=PIECES) as psum,
+        tc.psum_pool(name="psum_picked", bufs=PIECES) as psum_picked,
+        tc.psum_pool(name="psum_placed", bufs=2) as psum_placed,
+        tc.psum_pool(name="psum_warm", bufs=1) as psum_warm,
     ):
         offsets = held.tile([P, N // 16], U16, name="offsets")
         nc.sync.dma_start(offsets[:], offs)
-        words = held.tile([P, WORDS], BF16, name="words")
-        nc.sync.dma_start(words[:], table)
         weights = held.tile([P, P], BF16, name="weights")
         nc.scalar.dma_start(weights[:], w)
-        code = held.tile([P, N], F32, name="code")
-        nc.scalar.dma_start(code[:], pos)
+        code = []
+        for c in range(PIECES):
+            code_c = held.tile([P, PIECE], F32, name=f"code{c}")
+            queue = nc.sync if c % 2 == 0 else nc.scalar
+            queue.dma_start(code_c[:], pos[:, c * PIECE : (c + 1) * PIECE])
+            code.append(code_c)
+        words = held.tile([P, WORDS], BF16, name="words")
+        nc.sync.dma_start(words[:], table)
         old_norm = held.tile([P, N // T], F32, name="old_norm")
-        nc.gpsimd.dma_start(old_norm[:], mem_norm)
+        nc.scalar.dma_start(old_norm[:], mem_norm)
         new_norm = held.tile([P, N // T], F32, name="new_norm")
 
-        scaled = []
+        zeros = held.tile([P, WARM_COLUMNS], BF16, name="zeros")
+        nc.vector.memset(zeros[:], 0.0)
+        warm = psum_warm.tile([P, WARM_COLUMNS], F32, name="warm")
+        for i in range(WARM_MATMULS):
+            nc.tensor.matmul(warm[:], zeros[:, 0:P], zeros[:], start=True, stop=True)
+
+        picked = []
         for c in range(PIECES):
-            picked = psum.tile([P, PIECE], F32, name="picked")
+            picked_c = psum_picked.tile([P, PIECE], F32, name="picked")
             piece_offsets = offsets[:, c * (PIECE // 16) : (c + 1) * (PIECE // 16)]
-            nc.tensor.matmul(picked[:], weights[:], words[:].indirect(piece_offsets), start=True, stop=True)
-            scaled_c = work.tile([P, PIECE], F32, name="scaled")
-            nc.scalar.mul(scaled_c[:], picked[:], SCALE)
-            scaled.append(scaled_c)
+            nc.tensor.matmul(picked_c[:], weights[:], words[:].indirect(piece_offsets), start=True, stop=True)
+            picked.append(picked_c)
+
+        placed = []
+        for c in range(PIECES):
+            code_bf = work.tile([P, PIECE], BF16, name="code_bf")
+            nc.vector.tensor_copy(code_bf[:], code[c][:])
+            placed_ps = psum_placed.tile([P, PIECE], F32, name="placed_ps")
+            nc.tensor.matmul(placed_ps[:], weights[:], code_bf[:], start=True, stop=True)
+            placed_c = work.tile([P, PIECE], F32, name="placed")
+            nc.scalar.copy(placed_c[:], placed_ps[:])
+            placed.append(placed_c)
+
+        values, decays = [], []
+        for c in range(PIECES):
+            v = work.tile([P, PIECE], F32, name="v")
+            nc.vector.scalar_tensor_tensor(v[:], picked[c][:], SCALE, placed[c][:], ALU.mult, ALU.add)
+            drop = work.tile([P, PIECE], F32, name="drop")
+            nc.scalar.activation(drop[:], v[:], ACT.Relu, scale=-1.0)
+            decayed = work.tile([P, PIECE], F32, name="decayed")
+            nc.scalar.activation(decayed[:], drop[:], ACT.Exp, scale=-1.0)
+            values.append(v)
+            decays.append(decayed)
 
         for c in range(PIECES):
-            entries = slice(c * PIECE, (c + 1) * PIECE)
             sequences = slice(c * (PIECE // T), (c + 1) * (PIECE // T))
-            code_bf = work.tile([P, PIECE], BF16, name="code_bf")
-            nc.vector.tensor_copy(code_bf[:], code[:, entries])
-            placed = psum.tile([P, PIECE], F32, name="placed")
-            nc.tensor.matmul(placed[:], weights[:], code_bf[:], start=True, stop=True)
-            v = work.tile([P, PIECE], F32, name="v")
-            nc.vector.tensor_tensor(v[:], scaled[c][:], placed[:], ALU.add)
-            below = work.tile([P, PIECE], F32, name="below")
-            nc.vector.tensor_scalar_min(below[:], v[:], 0.0)
-            decayed = work.tile([P, PIECE], F32, name="decayed")
-            nc.scalar.activation(decayed[:], below[:], ACT.Exp)
             feature = work.tile([P, PIECE], F32, name="feature")
-            nc.vector.scalar_tensor_tensor(feature[:], v[:], 0.0, decayed[:], ALU.max, ALU.add)
+            nc.vector.scalar_tensor_tensor(feature[:], values[c][:], 0.0, decays[c][:], ALU.max, ALU.add)
             summed = work.tile([P, PIECE // T], F32, name="summed")
             nc.vector.tensor_reduce(
                 out=summed[:],

@@ -13,8 +13,6 @@ T = 8
 PIECE = 256
 PIECES = N // PIECE
 SCALE = math.sqrt(128.0)
-WARM_COLUMNS = 512
-WARM_MATMULS = 5
 
 FLOPS = 2 * (2 * P * P * N)
 
@@ -26,7 +24,6 @@ def tile_infiniattentionlm_kernel(tc, table, w, pos, mem_norm, offs, out):
         tc.tile_pool(name="work", bufs=PIECES) as work,
         tc.psum_pool(name="psum_picked", bufs=PIECES) as psum_picked,
         tc.psum_pool(name="psum_placed", bufs=2) as psum_placed,
-        tc.psum_pool(name="psum_warm", bufs=1) as psum_warm,
     ):
         offsets = held.tile([P, N // 16], U16, name="offsets")
         nc.sync.dma_start(offsets[:], offs)
@@ -43,12 +40,6 @@ def tile_infiniattentionlm_kernel(tc, table, w, pos, mem_norm, offs, out):
         old_norm = held.tile([P, N // T], F32, name="old_norm")
         nc.scalar.dma_start(old_norm[:], mem_norm)
         new_norm = held.tile([P, N // T], F32, name="new_norm")
-
-        zeros = held.tile([P, WARM_COLUMNS], BF16, name="zeros")
-        nc.vector.memset(zeros[:], 0.0)
-        warm = psum_warm.tile([P, WARM_COLUMNS], F32, name="warm")
-        for i in range(WARM_MATMULS):
-            nc.tensor.matmul(warm[:], zeros[:, 0:P], zeros[:], start=True, stop=True)
 
         picked = []
         for c in range(PIECES):

@@ -12,6 +12,7 @@ N = 1024
 T = 8
 PIECE = 256
 PIECES = N // PIECE
+SEQS = PIECE // T
 SCALE = math.sqrt(128.0)
 
 FLOPS = 2 * (2 * P * P * N)
@@ -23,63 +24,73 @@ def tile_infiniattentionlm_kernel(tc, table, w, pos, mem_norm, offs, out):
         tc.tile_pool(name="held", bufs=1) as held,
         tc.tile_pool(name="work", bufs=PIECES) as work,
         tc.psum_pool(name="psum_picked", bufs=PIECES) as psum_picked,
-        tc.psum_pool(name="psum_placed", bufs=2) as psum_placed,
+        tc.psum_pool(name="psum_placed", bufs=3) as psum_placed,
     ):
         offsets = held.tile([P, N // 16], U16, name="offsets")
-        nc.sync.dma_start(offsets[:], offs)
-        weights = held.tile([P, P], BF16, name="weights")
-        nc.scalar.dma_start(weights[:], w)
-        code = []
-        for c in range(PIECES):
-            code_c = held.tile([P, PIECE], F32, name=f"code{c}")
-            queue = nc.sync if c % 2 == 0 else nc.scalar
-            queue.dma_start(code_c[:], pos[:, c * PIECE : (c + 1) * PIECE])
-            code.append(code_c)
         words = held.tile([P, WORDS], BF16, name="words")
-        nc.sync.dma_start(words[:], table)
+        weights = held.tile([P, P], BF16, name="weights")
         old_norm = held.tile([P, N // T], F32, name="old_norm")
-        nc.scalar.dma_start(old_norm[:], mem_norm)
         new_norm = held.tile([P, N // T], F32, name="new_norm")
+        code = [held.tile([P, PIECE], F32, name=f"code{c}") for c in range(PIECES)]
+        terms = held.tile([P, N // T, T + 1], F32, name="terms")
 
-        picked = []
+        nc.scalar.dma_start(weights[:], w)
+        nc.sync.dma_start(offsets[:], offs)
+        nc.sync.dma_start(words[:], table)
+        nc.sync.dma_start(old_norm[:], mem_norm)
         for c in range(PIECES):
-            picked_c = psum_picked.tile([P, PIECE], F32, name="picked")
+            nc.sync.dma_start(code[c][:], pos[:, c * PIECE : (c + 1) * PIECE])
+
+        lifted = []
+        for c in range(PIECES):
+            picked = psum_picked.tile([P, PIECE], F32, name="picked")
             piece_offsets = offsets[:, c * (PIECE // 16) : (c + 1) * (PIECE // 16)]
-            nc.tensor.matmul(picked_c[:], weights[:], words[:].indirect(piece_offsets), start=True, stop=True)
-            picked.append(picked_c)
+            nc.tensor.matmul(picked[:], weights[:], words[:].indirect(piece_offsets), start=True, stop=True)
+            lifted_c = work.tile([P, PIECE], F32, name="lifted")
+            nc.scalar.activation(lifted_c[:], picked[:], ACT.Identity, bias=1.0, scale=SCALE)
+            lifted.append(lifted_c)
+
+        nc.vector.tensor_copy(terms[:, :, T : T + 1], old_norm[:].unsqueeze(2))
 
         placed = []
         for c in range(PIECES):
             code_bf = work.tile([P, PIECE], BF16, name="code_bf")
             nc.vector.tensor_copy(code_bf[:], code[c][:])
-            placed_ps = psum_placed.tile([P, PIECE], F32, name="placed_ps")
-            nc.tensor.matmul(placed_ps[:], weights[:], code_bf[:], start=True, stop=True)
-            placed_c = work.tile([P, PIECE], F32, name="placed")
-            nc.scalar.copy(placed_c[:], placed_ps[:])
+            placed_c = psum_placed.tile([P, PIECE], F32, name="placed")
+            nc.tensor.matmul(placed_c[:], weights[:], code_bf[:], start=True, stop=True)
             placed.append(placed_c)
 
-        values, decays = [], []
-        for c in range(PIECES):
-            v = work.tile([P, PIECE], F32, name="v")
-            nc.vector.scalar_tensor_tensor(v[:], picked[c][:], SCALE, placed[c][:], ALU.mult, ALU.add)
-            drop = work.tile([P, PIECE], F32, name="drop")
-            nc.scalar.activation(drop[:], v[:], ACT.Relu, scale=-1.0)
-            decayed = work.tile([P, PIECE], F32, name="decayed")
-            nc.scalar.activation(decayed[:], drop[:], ACT.Exp, scale=-1.0)
-            values.append(v)
-            decays.append(decayed)
+        values, growths = {}, {}
 
-        for c in range(PIECES):
-            sequences = slice(c * (PIECE // T), (c + 1) * (PIECE // T))
-            feature = work.tile([P, PIECE], F32, name="feature")
-            nc.vector.scalar_tensor_tensor(feature[:], values[c][:], 0.0, decays[c][:], ALU.max, ALU.add)
-            summed = work.tile([P, PIECE // T], F32, name="summed")
-            nc.vector.tensor_reduce(
-                out=summed[:],
-                in_=feature[:].rearrange("p (b t) -> p b t", t=T),
-                axis=mybir.AxisListType.X,
-                op=ALU.add,
+        def add_and_exp(c):
+            v1 = work.tile([P, PIECE], F32, name="v1")
+            nc.vector.tensor_tensor(v1[:], lifted[c][:], placed[c][:], ALU.add)
+            grown = work.tile([P, PIECE], F32, name="grown")
+            nc.scalar.activation(grown[:], v1[:], ACT.Exp, bias=-1.0)
+            values[c], growths[c] = v1, grown
+
+        def features(c):
+            nc.vector.scalar_tensor_tensor(
+                terms[:, c * SEQS : (c + 1) * SEQS, 0:T],
+                growths[c][:].rearrange("p (b t) -> p b t", t=T),
+                1.0,
+                values[c][:].rearrange("p (b t) -> p b t", t=T),
+                ALU.min,
+                ALU.max,
             )
-            nc.vector.tensor_tensor(new_norm[:, sequences], summed[:], old_norm[:, sequences], ALU.add)
+
+        def sums(c):
+            sequences = slice(c * SEQS, (c + 1) * SEQS)
+            nc.vector.tensor_reduce(
+                out=new_norm[:, sequences], in_=terms[:, sequences, :], axis=mybir.AxisListType.X, op=ALU.add
+            )
+
+        for step in range(PIECES + 3):
+            if step < PIECES:
+                add_and_exp(step)
+            if 0 <= step - 2 < PIECES:
+                features(step - 2)
+            if 0 <= step - 3 < PIECES:
+                sums(step - 3)
 
         nc.sync.dma_start(out, new_norm[:])

@@ -52,22 +52,19 @@ def tile_infiniattentionlm_kernel(tc, table, w, pos, mem_norm, offs, out):
 
         nc.vector.tensor_copy(terms[:, :, T : T + 1], old_norm[:].unsqueeze(2))
 
-        placed = []
-        for c in range(PIECES):
+        placed, values, growths = {}, {}, {}
+
+        def project(c):
             code_bf = work.tile([P, PIECE], BF16, name="code_bf")
             nc.vector.tensor_copy(code_bf[:], code[c][:])
-            placed_c = psum_placed.tile([P, PIECE], F32, name="placed")
-            nc.tensor.matmul(placed_c[:], weights[:], code_bf[:], start=True, stop=True)
-            placed.append(placed_c)
-
-        values, growths = {}, {}
+            placed[c] = psum_placed.tile([P, PIECE], F32, name="placed")
+            nc.tensor.matmul(placed[c][:], weights[:], code_bf[:], start=True, stop=True)
 
         def add_and_exp(c):
-            v1 = work.tile([P, PIECE], F32, name="v1")
-            nc.vector.tensor_tensor(v1[:], lifted[c][:], placed[c][:], ALU.add)
-            grown = work.tile([P, PIECE], F32, name="grown")
-            nc.scalar.activation(grown[:], v1[:], ACT.Exp, bias=-1.0)
-            values[c], growths[c] = v1, grown
+            values[c] = work.tile([P, PIECE], F32, name="v1")
+            nc.vector.tensor_tensor(values[c][:], lifted[c][:], placed[c][:], ALU.add)
+            growths[c] = work.tile([P, PIECE], F32, name="grown")
+            nc.scalar.activation(growths[c][:], values[c][:], ACT.Exp, bias=-1.0)
 
         def features(c):
             nc.vector.scalar_tensor_tensor(
@@ -85,12 +82,10 @@ def tile_infiniattentionlm_kernel(tc, table, w, pos, mem_norm, offs, out):
                 out=new_norm[:, sequences], in_=terms[:, sequences, :], axis=mybir.AxisListType.X, op=ALU.add
             )
 
-        for step in range(PIECES + 3):
-            if step < PIECES:
-                add_and_exp(step)
-            if 0 <= step - 2 < PIECES:
-                features(step - 2)
-            if 0 <= step - 3 < PIECES:
-                sums(step - 3)
+        stages = ((project, 0), (add_and_exp, 2), (features, 4), (sums, 5))
+        for step in range(PIECES + 5):
+            for stage, lag in stages:
+                if 0 <= step - lag < PIECES:
+                    stage(step - lag)
 
         nc.sync.dma_start(out, new_norm[:])

@@ -4,16 +4,20 @@ import concourse.mybir as mybir
 
 BF16, F32, U16 = mybir.dt.bfloat16, mybir.dt.float32, mybir.dt.uint16
 ALU = mybir.AluOpType
-ACT = mybir.ActivationFunctionType
+FUNC = mybir.ActivationFunctionType
 
 P = 128
 WORDS = 1024
 N = 1024
 T = 8
-PIECE = 256
-PIECES = N // PIECE
-SEQS = PIECE // T
 SCALE = math.sqrt(128.0)
+
+PIECES = 4
+PIECE = N // PIECES
+SEQS = PIECE // T
+
+FEATURES_LAG = 2
+SUMS_LAG = 3
 
 FLOPS = 2 * (2 * P * P * N)
 
@@ -23,8 +27,7 @@ def tile_infiniattentionlm_kernel(tc, table, w, pos, mem_norm, offs, out):
     with (
         tc.tile_pool(name="held", bufs=1) as held,
         tc.tile_pool(name="work", bufs=PIECES) as work,
-        tc.psum_pool(name="psum_picked", bufs=PIECES) as psum_picked,
-        tc.psum_pool(name="psum_placed", bufs=3) as psum_placed,
+        tc.psum_pool(name="psum", bufs=PIECES) as psum,
     ):
         offsets = held.tile([P, N // 16], U16, name="offsets")
         words = held.tile([P, WORDS], BF16, name="words")
@@ -43,35 +46,37 @@ def tile_infiniattentionlm_kernel(tc, table, w, pos, mem_norm, offs, out):
 
         lifted = []
         for c in range(PIECES):
-            picked = psum_picked.tile([P, PIECE], F32, name="picked")
+            picked = psum.tile([P, PIECE], F32, name="picked")
             piece_offsets = offsets[:, c * (PIECE // 16) : (c + 1) * (PIECE // 16)]
             nc.tensor.matmul(picked[:], weights[:], words[:].indirect(piece_offsets), start=True, stop=True)
             lifted_c = work.tile([P, PIECE], F32, name="lifted")
-            nc.scalar.activation(lifted_c[:], picked[:], ACT.Identity, bias=1.0, scale=SCALE)
+            nc.scalar.activation(lifted_c[:], picked[:], FUNC.Identity, bias=1.0, scale=SCALE)
             lifted.append(lifted_c)
+
+        placed = []
+        for c in range(PIECES):
+            code_bf = work.tile([P, PIECE], BF16, name="code_bf")
+            nc.gpsimd.tensor_copy(code_bf[:], code[c][:])
+            placed_c = psum.tile([P, PIECE], F32, name="placed")
+            nc.tensor.matmul(placed_c[:], weights[:], code_bf[:], start=True, stop=True)
+            placed.append(placed_c)
 
         nc.vector.tensor_copy(terms[:, :, T : T + 1], old_norm[:].unsqueeze(2))
 
-        placed, values, growths = {}, {}, {}
-
-        def project(c):
-            code_bf = work.tile([P, PIECE], BF16, name="code_bf")
-            nc.vector.tensor_copy(code_bf[:], code[c][:])
-            placed[c] = psum_placed.tile([P, PIECE], F32, name="placed")
-            nc.tensor.matmul(placed[c][:], weights[:], code_bf[:], start=True, stop=True)
+        v_plus_1, exp_v = {}, {}
 
         def add_and_exp(c):
-            values[c] = work.tile([P, PIECE], F32, name="v1")
-            nc.vector.tensor_tensor(values[c][:], lifted[c][:], placed[c][:], ALU.add)
-            growths[c] = work.tile([P, PIECE], F32, name="grown")
-            nc.scalar.activation(growths[c][:], values[c][:], ACT.Exp, bias=-1.0)
+            v_plus_1[c] = work.tile([P, PIECE], F32, name="v_plus_1")
+            nc.vector.tensor_tensor(v_plus_1[c][:], lifted[c][:], placed[c][:], ALU.add)
+            exp_v[c] = work.tile([P, PIECE], F32, name="exp_v")
+            nc.scalar.activation(exp_v[c][:], v_plus_1[c][:], FUNC.Exp, bias=-1.0)
 
         def features(c):
             nc.vector.scalar_tensor_tensor(
                 terms[:, c * SEQS : (c + 1) * SEQS, 0:T],
-                growths[c][:].rearrange("p (b t) -> p b t", t=T),
+                exp_v[c][:].rearrange("p (b t) -> p b t", t=T),
                 1.0,
-                values[c][:].rearrange("p (b t) -> p b t", t=T),
+                v_plus_1[c][:].rearrange("p (b t) -> p b t", t=T),
                 ALU.min,
                 ALU.max,
             )
@@ -82,10 +87,12 @@ def tile_infiniattentionlm_kernel(tc, table, w, pos, mem_norm, offs, out):
                 out=new_norm[:, sequences], in_=terms[:, sequences, :], axis=mybir.AxisListType.X, op=ALU.add
             )
 
-        stages = ((project, 0), (add_and_exp, 2), (features, 4), (sums, 5))
-        for step in range(PIECES + 5):
-            for stage, lag in stages:
-                if 0 <= step - lag < PIECES:
-                    stage(step - lag)
+        for step in range(PIECES + SUMS_LAG):
+            if step < PIECES:
+                add_and_exp(step)
+            if 0 <= step - FEATURES_LAG < PIECES:
+                features(step - FEATURES_LAG)
+            if 0 <= step - SUMS_LAG < PIECES:
+                sums(step - SUMS_LAG)
 
         nc.sync.dma_start(out, new_norm[:])

@@ -19,6 +19,8 @@ SEQS = PIECE // T
 FEATURES_LAG = 2
 SUMS_LAG = 3
 
+WARM_MATMULS = 8
+
 FLOPS = 2 * (2 * P * P * N)
 
 
@@ -43,6 +45,12 @@ def tile_infiniattentionlm_kernel(tc, table, w, pos, mem_norm, offs, out):
         nc.sync.dma_start(old_norm[:], mem_norm)
         for c in range(PIECES):
             nc.sync.dma_start(code[c][:], pos[:, c * PIECE : (c + 1) * PIECE])
+
+        zeros = held.tile([P, PIECE], BF16, name="zeros")
+        nc.vector.memset(zeros[:], 0.0)
+        warm = psum.tile([P, PIECE], F32, name="warm", tag="picked")
+        for i in range(WARM_MATMULS):
+            nc.tensor.matmul(warm[:], zeros[:, 0:P], zeros[:], start=True, stop=True)
 
         lifted = []
         for c in range(PIECES):

@@ -19,8 +19,6 @@ SEQS = PIECE // T
 FEATURES_LAG = 2
 SUMS_LAG = 3
 
-WARM_MATMULS = 8
-
 FLOPS = 2 * (2 * P * P * N)
 
 
@@ -39,18 +37,12 @@ def tile_infiniattentionlm_kernel(tc, table, w, pos, mem_norm, offs, out):
         code = [held.tile([P, PIECE], F32, name=f"code{c}") for c in range(PIECES)]
         terms = held.tile([P, N // T, T + 1], F32, name="terms")
 
-        nc.scalar.dma_start(weights[:], w)
+        nc.scalar.dma_start(words[:], table)
         nc.sync.dma_start(offsets[:], offs)
-        nc.sync.dma_start(words[:], table)
+        nc.sync.dma_start(weights[:], w)
         nc.sync.dma_start(old_norm[:], mem_norm)
         for c in range(PIECES):
             nc.sync.dma_start(code[c][:], pos[:, c * PIECE : (c + 1) * PIECE])
-
-        zeros = held.tile([P, PIECE], BF16, name="zeros")
-        nc.vector.memset(zeros[:], 0.0)
-        warm = psum.tile([P, PIECE], F32, name="warm", tag="picked")
-        for i in range(WARM_MATMULS):
-            nc.tensor.matmul(warm[:], zeros[:, 0:P], zeros[:], start=True, stop=True)
 
         lifted = []
         for c in range(PIECES):
@@ -94,6 +86,7 @@ def tile_infiniattentionlm_kernel(tc, table, w, pos, mem_norm, offs, out):
             nc.vector.tensor_reduce(
                 out=new_norm[:, sequences], in_=terms[:, sequences, :], axis=mybir.AxisListType.X, op=ALU.add
             )
+            nc.sync.dma_start(out[:, sequences], new_norm[:, sequences])
 
         for step in range(PIECES + SUMS_LAG):
             if step < PIECES:
@@ -102,5 +95,3 @@ def tile_infiniattentionlm_kernel(tc, table, w, pos, mem_norm, offs, out):
                 features(step - FEATURES_LAG)
             if 0 <= step - SUMS_LAG < PIECES:
                 sums(step - SUMS_LAG)
-
-        nc.sync.dma_start(out, new_norm[:])

@@ -16,6 +16,8 @@ PIECES = 4
 PIECE = N // PIECES
 SEQS = PIECE // T
 
+EARLY = 2
+
 FEATURES_LAG = 2
 SUMS_LAG = 3
 
@@ -37,29 +39,36 @@ def tile_infiniattentionlm_kernel(tc, table, w, pos, mem_norm, offs, out):
         code = [held.tile([P, PIECE], F32, name=f"code{c}") for c in range(PIECES)]
         terms = held.tile([P, N // T, T + 1], F32, name="terms")
 
-        nc.scalar.dma_start(words[:], table)
         nc.sync.dma_start(offsets[:], offs)
         nc.sync.dma_start(weights[:], w)
-        nc.sync.dma_start(old_norm[:], mem_norm)
-        for c in range(PIECES):
+        for c in range(EARLY):
             nc.sync.dma_start(code[c][:], pos[:, c * PIECE : (c + 1) * PIECE])
+        nc.sync.dma_start(words[:], table)
+        for c in range(EARLY, PIECES):
+            nc.sync.dma_start(code[c][:], pos[:, c * PIECE : (c + 1) * PIECE])
+        nc.sync.dma_start(old_norm[:], mem_norm)
 
-        lifted = []
-        for c in range(PIECES):
+        lifted, placed = {}, {}
+
+        def pick_and_lift(c):
             picked = psum.tile([P, PIECE], F32, name="picked")
             piece_offsets = offsets[:, c * (PIECE // 16) : (c + 1) * (PIECE // 16)]
             nc.tensor.matmul(picked[:], weights[:], words[:].indirect(piece_offsets), start=True, stop=True)
-            lifted_c = work.tile([P, PIECE], F32, name="lifted")
-            nc.scalar.activation(lifted_c[:], picked[:], FUNC.Identity, bias=1.0, scale=SCALE)
-            lifted.append(lifted_c)
+            lifted[c] = work.tile([P, PIECE], F32, name="lifted")
+            nc.scalar.activation(lifted[c][:], picked[:], FUNC.Identity, bias=1.0, scale=SCALE)
 
-        placed = []
-        for c in range(PIECES):
+        def round_and_place(c):
             code_bf = work.tile([P, PIECE], BF16, name="code_bf")
-            nc.gpsimd.tensor_copy(code_bf[:], code[c][:])
-            placed_c = psum.tile([P, PIECE], F32, name="placed")
-            nc.tensor.matmul(placed_c[:], weights[:], code_bf[:], start=True, stop=True)
-            placed.append(placed_c)
+            nc.vector.tensor_copy(code_bf[:], code[c][:])
+            placed[c] = psum.tile([P, PIECE], F32, name="placed")
+            nc.tensor.matmul(placed[c][:], weights[:], code_bf[:], start=True, stop=True)
+
+        for c in range(EARLY):
+            round_and_place(c)
+        for c in range(PIECES):
+            pick_and_lift(c)
+        for c in range(EARLY, PIECES):
+            round_and_place(c)
 
         nc.vector.tensor_copy(terms[:, :, T : T + 1], old_norm[:].unsqueeze(2))
 

@@ -16,11 +16,6 @@ PIECES = 4
 PIECE = N // PIECES
 SEQS = PIECE // T
 
-EARLY = 2
-
-FEATURES_LAG = 2
-SUMS_LAG = 3
-
 FLOPS = 2 * (2 * P * P * N)
 
 
@@ -39,68 +34,53 @@ def tile_infiniattentionlm_kernel(tc, table, w, pos, mem_norm, offs, out):
         code = [held.tile([P, PIECE], F32, name=f"code{c}") for c in range(PIECES)]
         terms = held.tile([P, N // T, T + 1], F32, name="terms")
 
-        nc.sync.dma_start(offsets[:], offs)
         nc.sync.dma_start(weights[:], w)
-        for c in range(EARLY):
+        for c in range(PIECES):
             nc.sync.dma_start(code[c][:], pos[:, c * PIECE : (c + 1) * PIECE])
+        nc.sync.dma_start(offsets[:], offs)
         nc.sync.dma_start(words[:], table)
-        for c in range(EARLY, PIECES):
-            nc.sync.dma_start(code[c][:], pos[:, c * PIECE : (c + 1) * PIECE])
         nc.sync.dma_start(old_norm[:], mem_norm)
 
-        lifted, placed = {}, {}
+        share = held.tile([P, P], BF16, name="share")
+        ones = held.tile([P, PIECE], BF16, name="ones")
+        nc.gpsimd.memset(share[:], 1.0 / P)
+        nc.gpsimd.memset(ones[:], 1.0)
+        v_plus_1 = [psum.tile([P, PIECE], F32, name="v_plus_1") for c in range(PIECES)]
+        for c in range(PIECES):
+            nc.tensor.matmul(v_plus_1[c][:], share[:], ones[:], start=True, stop=False)
 
-        def pick_and_lift(c):
-            picked = psum.tile([P, PIECE], F32, name="picked")
-            piece_offsets = offsets[:, c * (PIECE // 16) : (c + 1) * (PIECE // 16)]
-            nc.tensor.matmul(picked[:], weights[:], words[:].indirect(piece_offsets), start=True, stop=True)
-            lifted[c] = work.tile([P, PIECE], F32, name="lifted")
-            nc.scalar.activation(lifted[c][:], picked[:], FUNC.Identity, bias=1.0, scale=SCALE)
+        scaled = held.tile([P, P], F32, name="scaled")
+        scaled_high = held.tile([P, P], BF16, name="scaled_high")
+        scaled_low = held.tile([P, P], BF16, name="scaled_low")
+        nc.gpsimd.tensor_scalar_mul(scaled[:], weights[:], SCALE)
+        nc.gpsimd.tensor_copy(scaled_high[:], scaled[:])
+        nc.gpsimd.tensor_tensor(scaled_low[:], scaled[:], scaled_high[:], ALU.subtract)
 
-        def round_and_place(c):
+        for c in range(PIECES):
             code_bf = work.tile([P, PIECE], BF16, name="code_bf")
             nc.vector.tensor_copy(code_bf[:], code[c][:])
-            placed[c] = psum.tile([P, PIECE], F32, name="placed")
-            nc.tensor.matmul(placed[c][:], weights[:], code_bf[:], start=True, stop=True)
-
-        for c in range(EARLY):
-            round_and_place(c)
-        for c in range(PIECES):
-            pick_and_lift(c)
-        for c in range(EARLY, PIECES):
-            round_and_place(c)
+            nc.tensor.matmul(v_plus_1[c][:], weights[:], code_bf[:], start=False, stop=False)
 
         nc.vector.tensor_copy(terms[:, :, T : T + 1], old_norm[:].unsqueeze(2))
 
-        v_plus_1, exp_v = {}, {}
+        for c in range(PIECES):
+            looked_up = words[:].indirect(offsets[:, c * (PIECE // 16) : (c + 1) * (PIECE // 16)])
+            nc.tensor.matmul(v_plus_1[c][:], scaled_high[:], looked_up, start=False, stop=False)
+            nc.tensor.matmul(v_plus_1[c][:], scaled_low[:], looked_up, start=False, stop=True)
 
-        def add_and_exp(c):
-            v_plus_1[c] = work.tile([P, PIECE], F32, name="v_plus_1")
-            nc.vector.tensor_tensor(v_plus_1[c][:], lifted[c][:], placed[c][:], ALU.add)
-            exp_v[c] = work.tile([P, PIECE], F32, name="exp_v")
-            nc.scalar.activation(exp_v[c][:], v_plus_1[c][:], FUNC.Exp, bias=-1.0)
+            exp_v = work.tile([P, PIECE], F32, name="exp_v")
+            nc.scalar.activation(exp_v[:], v_plus_1[c][:], FUNC.Exp, bias=-1.0)
 
-        def features(c):
+            sequences = slice(c * SEQS, (c + 1) * SEQS)
             nc.vector.scalar_tensor_tensor(
-                terms[:, c * SEQS : (c + 1) * SEQS, 0:T],
-                exp_v[c][:].rearrange("p (b t) -> p b t", t=T),
+                terms[:, sequences, 0:T],
+                exp_v[:].rearrange("p (b t) -> p b t", t=T),
                 1.0,
                 v_plus_1[c][:].rearrange("p (b t) -> p b t", t=T),
                 ALU.min,
                 ALU.max,
             )
-
-        def sums(c):
-            sequences = slice(c * SEQS, (c + 1) * SEQS)
             nc.vector.tensor_reduce(
                 out=new_norm[:, sequences], in_=terms[:, sequences, :], axis=mybir.AxisListType.X, op=ALU.add
             )
             nc.sync.dma_start(out[:, sequences], new_norm[:, sequences])
-
-        for step in range(PIECES + SUMS_LAG):
-            if step < PIECES:
-                add_and_exp(step)
-            if 0 <= step - FEATURES_LAG < PIECES:
-                features(step - FEATURES_LAG)
-            if 0 <= step - SUMS_LAG < PIECES:
-                sums(step - SUMS_LAG)

@@ -49,17 +49,16 @@ def tile_infiniattentionlm_kernel(tc, table, w, pos, mem_norm, offs, out):
         for c in range(PIECES):
             nc.tensor.matmul(v_plus_1[c][:], share[:], ones[:], start=True, stop=False)
 
-        scaled = held.tile([P, P], F32, name="scaled")
         scaled_high = held.tile([P, P], BF16, name="scaled_high")
-        scaled_low = held.tile([P, P], BF16, name="scaled_low")
-        nc.gpsimd.tensor_scalar_mul(scaled[:], weights[:], SCALE)
-        nc.gpsimd.tensor_copy(scaled_high[:], scaled[:])
-        nc.gpsimd.tensor_tensor(scaled_low[:], scaled[:], scaled_high[:], ALU.subtract)
+        nc.scalar.activation(scaled_high[:], weights[:], FUNC.Identity, scale=SCALE)
 
         for c in range(PIECES):
             code_bf = work.tile([P, PIECE], BF16, name="code_bf")
             nc.vector.tensor_copy(code_bf[:], code[c][:])
             nc.tensor.matmul(v_plus_1[c][:], weights[:], code_bf[:], start=False, stop=False)
+
+        scaled_low = held.tile([P, P], BF16, name="scaled_low")
+        nc.vector.scalar_tensor_tensor(scaled_low[:], weights[:], SCALE, scaled_high[:], ALU.mult, ALU.subtract)
 
         nc.vector.tensor_copy(terms[:, :, T : T + 1], old_norm[:].unsqueeze(2))
 

@@ -43,8 +43,8 @@ def tile_infiniattentionlm_kernel(tc, table, w, pos, mem_norm, offs, out):
 
         share = held.tile([P, P], BF16, name="share")
         ones = held.tile([P, PIECE], BF16, name="ones")
-        nc.gpsimd.memset(share[:], 1.0 / P)
-        nc.gpsimd.memset(ones[:], 1.0)
+        nc.vector.memset(share[:], 1.0 / P)
+        nc.vector.memset(ones[:], 1.0)
         v_plus_1 = [psum.tile([P, PIECE], F32, name="v_plus_1") for c in range(PIECES)]
         for c in range(PIECES):
             nc.tensor.matmul(v_plus_1[c][:], share[:], ones[:], start=True, stop=False)
@@ -62,24 +62,34 @@ def tile_infiniattentionlm_kernel(tc, table, w, pos, mem_norm, offs, out):
 
         nc.vector.tensor_copy(terms[:, :, T : T + 1], old_norm[:].unsqueeze(2))
 
-        for c in range(PIECES):
+        def pick_and_exp(c):
             looked_up = words[:].indirect(offsets[:, c * (PIECE // 16) : (c + 1) * (PIECE // 16)])
             nc.tensor.matmul(v_plus_1[c][:], scaled_high[:], looked_up, start=False, stop=False)
             nc.tensor.matmul(v_plus_1[c][:], scaled_low[:], looked_up, start=False, stop=True)
+            exp_v[c] = work.tile([P, PIECE], F32, name="exp_v")
+            nc.scalar.activation(exp_v[c][:], v_plus_1[c][:], FUNC.Exp, bias=-1.0)
 
-            exp_v = work.tile([P, PIECE], F32, name="exp_v")
-            nc.scalar.activation(exp_v[:], v_plus_1[c][:], FUNC.Exp, bias=-1.0)
-
-            sequences = slice(c * SEQS, (c + 1) * SEQS)
+        def features(c):
             nc.vector.scalar_tensor_tensor(
-                terms[:, sequences, 0:T],
-                exp_v[:].rearrange("p (b t) -> p b t", t=T),
+                terms[:, c * SEQS : (c + 1) * SEQS, 0:T],
+                exp_v[c][:].rearrange("p (b t) -> p b t", t=T),
                 1.0,
                 v_plus_1[c][:].rearrange("p (b t) -> p b t", t=T),
                 ALU.min,
                 ALU.max,
             )
+
+        def sums(c):
+            sequences = slice(c * SEQS, (c + 1) * SEQS)
             nc.vector.tensor_reduce(
                 out=new_norm[:, sequences], in_=terms[:, sequences, :], axis=mybir.AxisListType.X, op=ALU.add
             )
             nc.sync.dma_start(out[:, sequences], new_norm[:, sequences])
+
+        exp_v = {}
+        for step in range(PIECES + 1):
+            if step < PIECES:
+                pick_and_exp(step)
+                features(step)
+            if step >= 1:
+                sums(step - 1)

@@ -11,6 +11,7 @@ WORDS = 1024
 N = 1024
 T = 8
 SCALE = math.sqrt(128.0)
+ROOM = 16
 
 PIECES = 4
 PIECE = N // PIECES
@@ -32,7 +33,7 @@ def tile_infiniattentionlm_kernel(tc, table, w, pos, mem_norm, offs, out):
         old_norm = held.tile([P, N // T], F32, name="old_norm")
         new_norm = held.tile([P, N // T], F32, name="new_norm")
         code = [held.tile([P, PIECE], F32, name=f"code{c}") for c in range(PIECES)]
-        terms = held.tile([P, N // T, T + 1], F32, name="terms")
+        terms = held.tile([P, N // T, ROOM], F32, name="terms")
 
         nc.sync.dma_start(weights[:], w)
         for c in range(PIECES):
@@ -82,7 +83,7 @@ def tile_infiniattentionlm_kernel(tc, table, w, pos, mem_norm, offs, out):
         def sums(c):
             sequences = slice(c * SEQS, (c + 1) * SEQS)
             nc.vector.tensor_reduce(
-                out=new_norm[:, sequences], in_=terms[:, sequences, :], axis=mybir.AxisListType.X, op=ALU.add
+                out=new_norm[:, sequences], in_=terms[:, sequences, 0 : T + 1], axis=mybir.AxisListType.X, op=ALU.add
             )
             nc.sync.dma_start(out[:, sequences], new_norm[:, sequences])
 

@@ -73,11 +73,11 @@ def tile_infiniattentionlm_kernel(tc, table, w, pos, mem_norm, offs, out):
         def features(c):
             nc.vector.scalar_tensor_tensor(
                 terms[:, c * SEQS : (c + 1) * SEQS, 0:T],
-                exp_v[c][:].rearrange("p (b t) -> p b t", t=T),
-                1.0,
                 v_plus_1[c][:].rearrange("p (b t) -> p b t", t=T),
-                ALU.min,
+                1.0,
+                exp_v[c][:].rearrange("p (b t) -> p b t", t=T),
                 ALU.max,
+                ALU.min,
             )
 
         def sums(c):

@@ -7,11 +7,14 @@ ALU = mybir.AluOpType
 FUNC = mybir.ActivationFunctionType
 
 P = 128
+HALF = P // 2
 WORDS = 1024
 N = 1024
 T = 8
 SCALE = math.sqrt(128.0)
-ROOM = 16
+UNIT = 1.0 / SCALE
+UNIT_HIGH = 181.0 / 2048.0
+UNIT_LOW = UNIT - UNIT_HIGH
 
 PIECES = 4
 PIECE = N // PIECES
@@ -33,64 +36,76 @@ def tile_infiniattentionlm_kernel(tc, table, w, pos, mem_norm, offs, out):
         old_norm = held.tile([P, N // T], F32, name="old_norm")
         new_norm = held.tile([P, N // T], F32, name="new_norm")
         code = [held.tile([P, PIECE], F32, name=f"code{c}") for c in range(PIECES)]
-        terms = held.tile([P, N // T, ROOM], F32, name="terms")
 
         nc.sync.dma_start(weights[:], w)
-        for c in range(PIECES):
-            nc.sync.dma_start(code[c][:], pos[:, c * PIECE : (c + 1) * PIECE])
+        nc.sync.dma_start(code[0][:], pos[:, 0:PIECE])
         nc.sync.dma_start(offsets[:], offs)
         nc.sync.dma_start(words[:], table)
+        for c in range(1, PIECES):
+            nc.sync.dma_start(code[c][:], pos[:, c * PIECE : (c + 1) * PIECE])
         nc.sync.dma_start(old_norm[:], mem_norm)
 
         share = held.tile([P, P], BF16, name="share")
-        ones = held.tile([P, PIECE], BF16, name="ones")
-        nc.vector.memset(share[:], 1.0 / P)
-        nc.vector.memset(ones[:], 1.0)
-        v_plus_1 = [psum.tile([P, PIECE], F32, name="v_plus_1") for c in range(PIECES)]
+        unit = held.tile([P, PIECE], BF16, name="unit")
+        nc.vector.memset(share[:], 1.0 / HALF)
+        nc.vector.memset(unit[0:HALF, :], UNIT_HIGH)
+        nc.vector.memset(unit[HALF:P, :], UNIT_LOW)
+        u = [psum.tile([P, PIECE], F32, name="u") for c in range(PIECES)]
         for c in range(PIECES):
-            nc.tensor.matmul(v_plus_1[c][:], share[:], ones[:], start=True, stop=False)
+            nc.tensor.matmul(u[c][:], share[:], unit[:], start=True, stop=False)
 
-        scaled_high = held.tile([P, P], BF16, name="scaled_high")
-        nc.scalar.activation(scaled_high[:], weights[:], FUNC.Identity, scale=SCALE)
+        high = held.tile([P, P], BF16, name="high")
+        low = held.tile([P, P], BF16, name="low")
+        nc.vector.tensor_scalar_mul(high[:], weights[:], UNIT)
+        nc.vector.scalar_tensor_tensor(low[:], weights[:], UNIT, high[:], ALU.mult, ALU.subtract)
 
-        for c in range(PIECES):
+        def add_code(c, stop):
             code_bf = work.tile([P, PIECE], BF16, name="code_bf")
             nc.vector.tensor_copy(code_bf[:], code[c][:])
-            nc.tensor.matmul(v_plus_1[c][:], weights[:], code_bf[:], start=False, stop=False)
+            nc.tensor.matmul(u[c][:], high[:], code_bf[:], start=False, stop=False)
+            nc.tensor.matmul(u[c][:], low[:], code_bf[:], start=False, stop=stop)
 
-        scaled_low = held.tile([P, P], BF16, name="scaled_low")
-        nc.vector.scalar_tensor_tensor(scaled_low[:], weights[:], SCALE, scaled_high[:], ALU.mult, ALU.subtract)
-
-        nc.vector.tensor_copy(terms[:, :, T : T + 1], old_norm[:].unsqueeze(2))
-
-        def pick_and_exp(c):
+        def look_up(c, stop):
             looked_up = words[:].indirect(offsets[:, c * (PIECE // 16) : (c + 1) * (PIECE // 16)])
-            nc.tensor.matmul(v_plus_1[c][:], scaled_high[:], looked_up, start=False, stop=False)
-            nc.tensor.matmul(v_plus_1[c][:], scaled_low[:], looked_up, start=False, stop=True)
+            nc.tensor.matmul(u[c][:], weights[:], looked_up, start=False, stop=stop)
+
+        def exponential(c):
             exp_v[c] = work.tile([P, PIECE], F32, name="exp_v")
-            nc.scalar.activation(exp_v[c][:], v_plus_1[c][:], FUNC.Exp, bias=-1.0)
+            nc.scalar.activation(exp_v[c][:], u[c][:], FUNC.Exp, bias=-1.0 - math.log(SCALE), scale=SCALE)
 
         def features(c):
-            nc.vector.scalar_tensor_tensor(
-                terms[:, c * SEQS : (c + 1) * SEQS, 0:T],
-                v_plus_1[c][:].rearrange("p (b t) -> p b t", t=T),
-                1.0,
-                exp_v[c][:].rearrange("p (b t) -> p b t", t=T),
-                ALU.max,
-                ALU.min,
-            )
+            feature[c] = work.tile([P, PIECE], F32, name="feature")
+            nc.vector.scalar_tensor_tensor(feature[c][:], u[c][:], UNIT, exp_v[c][:], ALU.max, ALU.min)
 
         def sums(c):
-            sequences = slice(c * SEQS, (c + 1) * SEQS)
+            total[c] = work.tile([P, SEQS], F32, name="total")
             nc.vector.tensor_reduce(
-                out=new_norm[:, sequences], in_=terms[:, sequences, 0 : T + 1], axis=mybir.AxisListType.X, op=ALU.add
+                out=total[c][:],
+                in_=feature[c][:].rearrange("p (b t) -> p b t", t=T),
+                axis=mybir.AxisListType.X,
+                op=ALU.add,
+            )
+
+        def update(c):
+            sequences = slice(c * SEQS, (c + 1) * SEQS)
+            nc.vector.scalar_tensor_tensor(
+                new_norm[:, sequences], total[c][:], SCALE, old_norm[:, sequences], ALU.mult, ALU.add
             )
             nc.sync.dma_start(out[:, sequences], new_norm[:, sequences])
 
-        exp_v = {}
-        for step in range(PIECES + 1):
+        exp_v, feature, total = {}, {}, {}
+        add_code(0, stop=False)
+        look_up(0, stop=True)
+        for c in range(1, PIECES):
+            look_up(c, stop=False)
+
+        for step in range(PIECES + 2):
             if step < PIECES:
-                pick_and_exp(step)
+                if step >= 1:
+                    add_code(step, stop=True)
+                exponential(step)
                 features(step)
-            if step >= 1:
+            if 1 <= step <= PIECES:
                 sums(step - 1)
+            if step >= 2:
+                update(step - 2)

@@ -17,6 +17,7 @@ UNIT_HIGH = 181.0 / 2048.0
 UNIT_LOW = UNIT - UNIT_HIGH
 
 PIECES = 4
+EARLY = 2
 PIECE = N // PIECES
 SEQS = PIECE // T
 
@@ -34,14 +35,15 @@ def tile_infiniattentionlm_kernel(tc, table, w, pos, mem_norm, offs, out):
         words = held.tile([P, WORDS], BF16, name="words")
         weights = held.tile([P, P], BF16, name="weights")
         old_norm = held.tile([P, N // T], F32, name="old_norm")
+        total = held.tile([P, N // T], F32, name="total")
         new_norm = held.tile([P, N // T], F32, name="new_norm")
         code = [held.tile([P, PIECE], F32, name=f"code{c}") for c in range(PIECES)]
 
         nc.sync.dma_start(weights[:], w)
-        nc.sync.dma_start(code[0][:], pos[:, 0:PIECE])
-        nc.sync.dma_start(offsets[:], offs)
-        nc.sync.dma_start(words[:], table)
-        for c in range(1, PIECES):
+        for c in range(PIECES):
+            if c == EARLY:
+                nc.sync.dma_start(offsets[:], offs)
+                nc.sync.dma_start(words[:], table)
             nc.sync.dma_start(code[c][:], pos[:, c * PIECE : (c + 1) * PIECE])
         nc.sync.dma_start(old_norm[:], mem_norm)
 
@@ -78,34 +80,34 @@ def tile_infiniattentionlm_kernel(tc, table, w, pos, mem_norm, offs, out):
             nc.vector.scalar_tensor_tensor(feature[c][:], u[c][:], UNIT, exp_v[c][:], ALU.max, ALU.min)
 
         def sums(c):
-            total[c] = work.tile([P, SEQS], F32, name="total")
             nc.vector.tensor_reduce(
-                out=total[c][:],
+                out=total[:, c * SEQS : (c + 1) * SEQS],
                 in_=feature[c][:].rearrange("p (b t) -> p b t", t=T),
                 axis=mybir.AxisListType.X,
                 op=ALU.add,
             )
 
-        def update(c):
-            sequences = slice(c * SEQS, (c + 1) * SEQS)
+        def update(first, end):
+            sequences = slice(first * SEQS, end * SEQS)
             nc.vector.scalar_tensor_tensor(
-                new_norm[:, sequences], total[c][:], SCALE, old_norm[:, sequences], ALU.mult, ALU.add
+                new_norm[:, sequences], total[:, sequences], SCALE, old_norm[:, sequences], ALU.mult, ALU.add
             )
             nc.sync.dma_start(out[:, sequences], new_norm[:, sequences])
 
-        exp_v, feature, total = {}, {}, {}
-        add_code(0, stop=False)
-        look_up(0, stop=True)
-        for c in range(1, PIECES):
-            look_up(c, stop=False)
+        exp_v, feature = {}, {}
+        for c in range(EARLY):
+            add_code(c, stop=False)
+        for c in range(PIECES):
+            look_up(c, stop=c < EARLY)
 
-        for step in range(PIECES + 2):
+        for step in range(PIECES + 1):
             if step < PIECES:
-                if step >= 1:
+                if step >= EARLY:
                     add_code(step, stop=True)
                 exponential(step)
                 features(step)
             if 1 <= step <= PIECES:
                 sums(step - 1)
-            if step >= 2:
-                update(step - 2)
+            if step == PIECES:
+                update(0, PIECES - 1)
+        update(PIECES - 1, PIECES)

@@ -37,14 +37,14 @@ def tile_infiniattentionlm_kernel(tc, table, w, pos, mem_norm, offs, out):
         old_norm = held.tile([P, N // T], F32, name="old_norm")
         total = held.tile([P, N // T], F32, name="total")
         new_norm = held.tile([P, N // T], F32, name="new_norm")
-        code = [held.tile([P, PIECE], F32, name=f"code{c}") for c in range(PIECES)]
+        early_code = held.tile([P, EARLY * PIECE], F32, name="early_code")
+        late_code = held.tile([P, N - EARLY * PIECE], F32, name="late_code")
 
         nc.sync.dma_start(weights[:], w)
-        for c in range(PIECES):
-            if c == EARLY:
-                nc.sync.dma_start(offsets[:], offs)
-                nc.sync.dma_start(words[:], table)
-            nc.sync.dma_start(code[c][:], pos[:, c * PIECE : (c + 1) * PIECE])
+        nc.sync.dma_start(early_code[:], pos[:, 0 : EARLY * PIECE])
+        nc.sync.dma_start(offsets[:], offs)
+        nc.sync.dma_start(words[:], table)
+        nc.sync.dma_start(late_code[:], pos[:, EARLY * PIECE : N])
         nc.sync.dma_start(old_norm[:], mem_norm)
 
         share = held.tile([P, P], BF16, name="share")
@@ -63,7 +63,8 @@ def tile_infiniattentionlm_kernel(tc, table, w, pos, mem_norm, offs, out):
 
         def add_code(c, stop):
             code_bf = work.tile([P, PIECE], BF16, name="code_bf")
-            nc.vector.tensor_copy(code_bf[:], code[c][:])
+            half, place = (early_code, c) if c < EARLY else (late_code, c - EARLY)
+            nc.vector.tensor_copy(code_bf[:], half[:, place * PIECE : (place + 1) * PIECE])
             nc.tensor.matmul(u[c][:], high[:], code_bf[:], start=False, stop=False)
             nc.tensor.matmul(u[c][:], low[:], code_bf[:], start=False, stop=stop)
 

@@ -7,7 +7,6 @@ ALU = mybir.AluOpType
 FUNC = mybir.ActivationFunctionType
 
 P = 128
-HALF = P // 2
 WORDS = 1024
 N = 1024
 T = 8
@@ -48,13 +47,15 @@ def tile_infiniattentionlm_kernel(tc, table, w, pos, mem_norm, offs, out):
         nc.sync.dma_start(old_norm[:], mem_norm)
 
         share = held.tile([P, P], BF16, name="share")
-        unit = held.tile([P, PIECE], BF16, name="unit")
-        nc.vector.memset(share[:], 1.0 / HALF)
-        nc.vector.memset(unit[0:HALF, :], UNIT_HIGH)
-        nc.vector.memset(unit[HALF:P, :], UNIT_LOW)
+        unit = held.tile([P, 2], BF16, name="unit")
+        nc.vector.memset(share[:], 1.0 / P)
+        nc.vector.memset(unit[:, 0:1], UNIT_HIGH)
+        nc.vector.memset(unit[:, 1:2], UNIT_LOW)
         u = [psum.tile([P, PIECE], F32, name="u") for c in range(PIECES)]
-        for c in range(PIECES):
-            nc.tensor.matmul(u[c][:], share[:], unit[:], start=True, stop=False)
+        for part in range(2):
+            for c in range(PIECES):
+                every_entry = unit[:, part : part + 1].to_broadcast([P, PIECE])
+                nc.tensor.matmul(u[c][:], share[:], every_entry, start=part == 0, stop=False)
 
         high = held.tile([P, P], BF16, name="high")
         low = held.tile([P, P], BF16, name="low")

@@ -15,10 +15,12 @@ UNIT = 1.0 / SCALE
 UNIT_HIGH = 181.0 / 2048.0
 UNIT_LOW = UNIT - UNIT_HIGH
 
-PIECES = 4
-EARLY = 2
-PIECE = N // PIECES
-SEQS = PIECE // T
+NARROW, WIDE = 128, 256
+WIDTHS = (NARROW, NARROW, WIDE, WIDE, WIDE)
+PIECES = len(WIDTHS)
+STARTS = tuple(sum(WIDTHS[:c]) for c in range(PIECES))
+EARLY = 3
+EARLY_N = STARTS[EARLY]
 
 FLOPS = 2 * (2 * P * P * N)
 
@@ -36,14 +38,14 @@ def tile_infiniattentionlm_kernel(tc, table, w, pos, mem_norm, offs, out):
         old_norm = held.tile([P, N // T], F32, name="old_norm")
         total = held.tile([P, N // T], F32, name="total")
         new_norm = held.tile([P, N // T], F32, name="new_norm")
-        early_code = held.tile([P, EARLY * PIECE], F32, name="early_code")
-        late_code = held.tile([P, N - EARLY * PIECE], F32, name="late_code")
+        early_code = held.tile([P, EARLY_N], F32, name="early_code")
+        late_code = held.tile([P, N - EARLY_N], F32, name="late_code")
 
         nc.sync.dma_start(weights[:], w)
-        nc.sync.dma_start(early_code[:], pos[:, 0 : EARLY * PIECE])
+        nc.sync.dma_start(early_code[:], pos[:, 0:EARLY_N])
         nc.sync.dma_start(offsets[:], offs)
         nc.sync.dma_start(words[:], table)
-        nc.sync.dma_start(late_code[:], pos[:, EARLY * PIECE : N])
+        nc.sync.dma_start(late_code[:], pos[:, EARLY_N:N])
         nc.sync.dma_start(old_norm[:], mem_norm)
 
         share = held.tile([P, P], BF16, name="share")
@@ -51,10 +53,10 @@ def tile_infiniattentionlm_kernel(tc, table, w, pos, mem_norm, offs, out):
         nc.vector.memset(share[:], 1.0 / P)
         nc.vector.memset(unit[:, 0:1], UNIT_HIGH)
         nc.vector.memset(unit[:, 1:2], UNIT_LOW)
-        u = [psum.tile([P, PIECE], F32, name="u") for c in range(PIECES)]
+        u = [psum.tile([P, WIDTHS[c]], F32, name="u") for c in range(PIECES)]
         for part in range(2):
             for c in range(PIECES):
-                every_entry = unit[:, part : part + 1].to_broadcast([P, PIECE])
+                every_entry = unit[:, part : part + 1].to_broadcast([P, WIDTHS[c]])
                 nc.tensor.matmul(u[c][:], share[:], every_entry, start=part == 0, stop=False)
 
         high = held.tile([P, P], BF16, name="high")
@@ -63,34 +65,34 @@ def tile_infiniattentionlm_kernel(tc, table, w, pos, mem_norm, offs, out):
         nc.vector.scalar_tensor_tensor(low[:], weights[:], UNIT, high[:], ALU.mult, ALU.subtract)
 
         def add_code(c, stop):
-            code_bf = work.tile([P, PIECE], BF16, name="code_bf")
-            half, place = (early_code, c) if c < EARLY else (late_code, c - EARLY)
-            nc.vector.tensor_copy(code_bf[:], half[:, place * PIECE : (place + 1) * PIECE])
+            code_bf = work.tile([P, WIDTHS[c]], BF16, name="code_bf")
+            half, first = (early_code, STARTS[c]) if c < EARLY else (late_code, STARTS[c] - EARLY_N)
+            nc.vector.tensor_copy(code_bf[:], half[:, first : first + WIDTHS[c]])
             nc.tensor.matmul(u[c][:], high[:], code_bf[:], start=False, stop=False)
             nc.tensor.matmul(u[c][:], low[:], code_bf[:], start=False, stop=stop)
 
         def look_up(c, stop):
-            looked_up = words[:].indirect(offsets[:, c * (PIECE // 16) : (c + 1) * (PIECE // 16)])
+            looked_up = words[:].indirect(offsets[:, STARTS[c] // 16 : (STARTS[c] + WIDTHS[c]) // 16])
             nc.tensor.matmul(u[c][:], weights[:], looked_up, start=False, stop=stop)
 
         def exponential(c):
-            exp_v[c] = work.tile([P, PIECE], F32, name="exp_v")
+            exp_v[c] = work.tile([P, WIDTHS[c]], F32, name="exp_v")
             nc.scalar.activation(exp_v[c][:], u[c][:], FUNC.Exp, bias=-1.0 - math.log(SCALE), scale=SCALE)
 
         def features(c):
-            feature[c] = work.tile([P, PIECE], F32, name="feature")
+            feature[c] = work.tile([P, WIDTHS[c]], F32, name="feature")
             nc.vector.scalar_tensor_tensor(feature[c][:], u[c][:], UNIT, exp_v[c][:], ALU.max, ALU.min)
 
         def sums(c):
             nc.vector.tensor_reduce(
-                out=total[:, c * SEQS : (c + 1) * SEQS],
+                out=total[:, STARTS[c] // T : (STARTS[c] + WIDTHS[c]) // T],
                 in_=feature[c][:].rearrange("p (b t) -> p b t", t=T),
                 axis=mybir.AxisListType.X,
                 op=ALU.add,
             )
 
         def update(first, end):
-            sequences = slice(first * SEQS, end * SEQS)
+            sequences = slice(STARTS[first] // T, (STARTS[end - 1] + WIDTHS[end - 1]) // T)
             nc.vector.scalar_tensor_tensor(
                 new_norm[:, sequences], total[:, sequences], SCALE, old_norm[:, sequences], ALU.mult, ALU.add
             )

@@ -21,6 +21,9 @@ PIECES = len(WIDTHS)
 STARTS = tuple(sum(WIDTHS[:c]) for c in range(PIECES))
 EARLY = 3
 EARLY_N = STARTS[EARLY]
+LAST = PIECES - 1
+DIVIDED_SEQS = STARTS[LAST] // T
+ROOM = 16
 
 FLOPS = 2 * (2 * P * P * N)
 
@@ -37,6 +40,7 @@ def tile_infiniattentionlm_kernel(tc, table, w, pos, mem_norm, offs, out):
         weights = held.tile([P, P], BF16, name="weights")
         old_norm = held.tile([P, N // T], F32, name="old_norm")
         total = held.tile([P, N // T], F32, name="total")
+        terms = held.tile([P, WIDTHS[LAST] // T, ROOM], F32, name="terms")
         new_norm = held.tile([P, N // T], F32, name="new_norm")
         early_code = held.tile([P, EARLY_N], F32, name="early_code")
         late_code = held.tile([P, N - EARLY_N], F32, name="late_code")
@@ -75,26 +79,46 @@ def tile_infiniattentionlm_kernel(tc, table, w, pos, mem_norm, offs, out):
             looked_up = words[:].indirect(offsets[:, STARTS[c] // 16 : (STARTS[c] + WIDTHS[c]) // 16])
             nc.tensor.matmul(u[c][:], weights[:], looked_up, start=False, stop=stop)
 
-        def exponential(c):
+        def by_sequence(ap):
+            return ap.rearrange("p (b t) -> p b t", t=T)
+
+        def divided_exponential(c):
             exp_v[c] = work.tile([P, WIDTHS[c]], F32, name="exp_v")
             nc.scalar.activation(exp_v[c][:], u[c][:], FUNC.Exp, bias=-1.0 - math.log(SCALE), scale=SCALE)
 
-        def features(c):
+        def divided_features(c):
             feature[c] = work.tile([P, WIDTHS[c]], F32, name="feature")
             nc.vector.scalar_tensor_tensor(feature[c][:], u[c][:], UNIT, exp_v[c][:], ALU.max, ALU.min)
 
-        def sums(c):
+        def divided_sums(c):
             nc.vector.tensor_reduce(
                 out=total[:, STARTS[c] // T : (STARTS[c] + WIDTHS[c]) // T],
-                in_=feature[c][:].rearrange("p (b t) -> p b t", t=T),
+                in_=by_sequence(feature[c][:]),
                 axis=mybir.AxisListType.X,
                 op=ALU.add,
             )
 
-        def update(first, end):
-            sequences = slice(STARTS[first] // T, (STARTS[end - 1] + WIDTHS[end - 1]) // T)
+        def update():
+            sequences = slice(0, DIVIDED_SEQS)
             nc.vector.scalar_tensor_tensor(
                 new_norm[:, sequences], total[:, sequences], SCALE, old_norm[:, sequences], ALU.mult, ALU.add
+            )
+            nc.sync.dma_start(out[:, sequences], new_norm[:, sequences])
+
+        def whole_exponential():
+            whole_exp = held.tile([P, WIDTHS[LAST]], F32, name="whole_exp")
+            above = held.tile([P, WIDTHS[LAST]], F32, name="above")
+            nc.scalar.activation(whole_exp[:], u[LAST][:], FUNC.Exp, bias=-1.0, scale=SCALE)
+            nc.scalar.activation(above[:], u[LAST][:], FUNC.Relu, bias=-1.0, scale=SCALE)
+            return by_sequence(whole_exp[:]), by_sequence(above[:])
+
+        def whole_features(exponential, above):
+            nc.vector.scalar_tensor_tensor(terms[:, :, 0:T], exponential, 1.0, above, ALU.min, ALU.add)
+
+        def whole_sums():
+            sequences = slice(DIVIDED_SEQS, N // T)
+            nc.vector.tensor_reduce(
+                out=new_norm[:, sequences], in_=terms[:, :, 0 : T + 1], axis=mybir.AxisListType.X, op=ALU.add
             )
             nc.sync.dma_start(out[:, sequences], new_norm[:, sequences])
 
@@ -104,14 +128,16 @@ def tile_infiniattentionlm_kernel(tc, table, w, pos, mem_norm, offs, out):
         for c in range(PIECES):
             look_up(c, stop=c < EARLY)
 
-        for step in range(PIECES + 1):
-            if step < PIECES:
-                if step >= EARLY:
-                    add_code(step, stop=True)
-                exponential(step)
-                features(step)
-            if 1 <= step <= PIECES:
-                sums(step - 1)
-            if step == PIECES:
-                update(0, PIECES - 1)
-        update(PIECES - 1, PIECES)
+        nc.vector.tensor_copy(terms[:, :, T : T + 1], old_norm[:, DIVIDED_SEQS:].unsqueeze(2))
+        for c in range(LAST):
+            if c >= EARLY:
+                add_code(c, stop=True)
+            divided_exponential(c)
+            divided_features(c)
+            if c >= 1:
+                divided_sums(c - 1)
+        add_code(LAST, stop=True)
+        whole_features(*whole_exponential())
+        divided_sums(LAST - 1)
+        update()
+        whole_sums()

import math

import concourse.mybir as mybir

BF16, F32, U16 = mybir.dt.bfloat16, mybir.dt.float32, mybir.dt.uint16
ALU = mybir.AluOpType
FUNC = mybir.ActivationFunctionType

P = 128
WORDS = 1024
N = 1024
T = 8
SCALE = math.sqrt(128.0)
UNIT = 1.0 / SCALE
UNIT_HIGH = 181.0 / 2048.0
UNIT_LOW = UNIT - UNIT_HIGH

NARROW, WIDE = 128, 256
WIDTHS = (NARROW, NARROW, WIDE, WIDE, WIDE)
PIECES = len(WIDTHS)
STARTS = tuple(sum(WIDTHS[:c]) for c in range(PIECES))
EARLY = 3
EARLY_N = STARTS[EARLY]
LAST = PIECES - 1
DIVIDED_SEQS = STARTS[LAST] // T
ROOM = 16

FLOPS = 2 * (2 * P * P * N)


def tile_infiniattentionlm_kernel(tc, table, w, pos, mem_norm, offs, out):
    nc = tc.nc
    with (
        tc.tile_pool(name="held", bufs=1) as held,
        tc.tile_pool(name="work", bufs=PIECES) as work,
        tc.psum_pool(name="psum", bufs=PIECES) as psum,
    ):
        offsets = held.tile([P, N // 16], U16, name="offsets")
        words = held.tile([P, WORDS], BF16, name="words")
        weights = held.tile([P, P], BF16, name="weights")
        old_norm = held.tile([P, N // T], F32, name="old_norm")
        total = held.tile([P, N // T], F32, name="total")
        terms = held.tile([P, WIDTHS[LAST] // T, ROOM], F32, name="terms")
        new_norm = held.tile([P, N // T], F32, name="new_norm")
        early_code = held.tile([P, EARLY_N], F32, name="early_code")
        late_code = held.tile([P, N - EARLY_N], F32, name="late_code")

        nc.sync.dma_start(weights[:], w)
        nc.sync.dma_start(early_code[:], pos[:, 0:EARLY_N])
        nc.sync.dma_start(offsets[:], offs)
        nc.sync.dma_start(words[:], table)
        nc.sync.dma_start(late_code[:], pos[:, EARLY_N:N])
        nc.sync.dma_start(old_norm[:], mem_norm)

        share = held.tile([P, P], BF16, name="share")
        unit = held.tile([P, 2], BF16, name="unit")
        nc.vector.memset(share[:], 1.0 / P)
        nc.vector.memset(unit[:, 0:1], UNIT_HIGH)
        nc.vector.memset(unit[:, 1:2], UNIT_LOW)
        u = [psum.tile([P, WIDTHS[c]], F32, name="u") for c in range(PIECES)]
        for part in range(2):
            for c in range(PIECES):
                every_entry = unit[:, part : part + 1].to_broadcast([P, WIDTHS[c]])
                nc.tensor.matmul(u[c][:], share[:], every_entry, start=part == 0, stop=False)

        high = held.tile([P, P], BF16, name="high")
        low = held.tile([P, P], BF16, name="low")
        nc.vector.tensor_scalar_mul(high[:], weights[:], UNIT)
        nc.vector.scalar_tensor_tensor(low[:], weights[:], UNIT, high[:], ALU.mult, ALU.subtract)

        def add_code(c, stop):
            code_bf = work.tile([P, WIDTHS[c]], BF16, name="code_bf")
            half, first = (early_code, STARTS[c]) if c < EARLY else (late_code, STARTS[c] - EARLY_N)
            nc.vector.tensor_copy(code_bf[:], half[:, first : first + WIDTHS[c]])
            nc.tensor.matmul(u[c][:], high[:], code_bf[:], start=False, stop=False)
            nc.tensor.matmul(u[c][:], low[:], code_bf[:], start=False, stop=stop)

        def look_up(c, stop):
            looked_up = words[:].indirect(offsets[:, STARTS[c] // 16 : (STARTS[c] + WIDTHS[c]) // 16])
            nc.tensor.matmul(u[c][:], weights[:], looked_up, start=False, stop=stop)

        def by_sequence(ap):
            return ap.rearrange("p (b t) -> p b t", t=T)

        def divided_exponential(c):
            exp_v[c] = work.tile([P, WIDTHS[c]], F32, name="exp_v")
            nc.scalar.activation(exp_v[c][:], u[c][:], FUNC.Exp, bias=-1.0 - math.log(SCALE), scale=SCALE)

        def divided_features(c):
            feature[c] = work.tile([P, WIDTHS[c]], F32, name="feature")
            nc.vector.scalar_tensor_tensor(feature[c][:], u[c][:], UNIT, exp_v[c][:], ALU.max, ALU.min)

        def divided_sums(c):
            nc.vector.tensor_reduce(
                out=total[:, STARTS[c] // T : (STARTS[c] + WIDTHS[c]) // T],
                in_=by_sequence(feature[c][:]),
                axis=mybir.AxisListType.X,
                op=ALU.add,
            )

        def update():
            sequences = slice(0, DIVIDED_SEQS)
            nc.vector.scalar_tensor_tensor(
                new_norm[:, sequences], total[:, sequences], SCALE, old_norm[:, sequences], ALU.mult, ALU.add
            )
            nc.sync.dma_start(out[:, sequences], new_norm[:, sequences])

        def whole_exponential():
            whole_exp = held.tile([P, WIDTHS[LAST]], F32, name="whole_exp")
            above = held.tile([P, WIDTHS[LAST]], F32, name="above")
            nc.scalar.activation(whole_exp[:], u[LAST][:], FUNC.Exp, bias=-1.0, scale=SCALE)
            nc.scalar.activation(above[:], u[LAST][:], FUNC.Relu, bias=-1.0, scale=SCALE)
            return by_sequence(whole_exp[:]), by_sequence(above[:])

        def whole_features(exponential, above):
            nc.vector.scalar_tensor_tensor(terms[:, :, 0:T], exponential, 1.0, above, ALU.min, ALU.add)

        def whole_sums():
            sequences = slice(DIVIDED_SEQS, N // T)
            nc.vector.tensor_reduce(
                out=new_norm[:, sequences], in_=terms[:, :, 0 : T + 1], axis=mybir.AxisListType.X, op=ALU.add
            )
            nc.sync.dma_start(out[:, sequences], new_norm[:, sequences])

        exp_v, feature = {}, {}
        for c in range(EARLY):
            add_code(c, stop=False)
        for c in range(PIECES):
            look_up(c, stop=c < EARLY)

        nc.vector.tensor_copy(terms[:, :, T : T + 1], old_norm[:, DIVIDED_SEQS:].unsqueeze(2))
        for c in range(LAST):
            if c >= EARLY:
                add_code(c, stop=True)
            divided_exponential(c)
            divided_features(c)
            if c >= 1:
                divided_sums(c - 1)
        add_code(LAST, stop=True)
        whole_features(*whole_exponential())
        divided_sums(LAST - 1)
        update()
        whole_sums()
